import numpy as np
import ml_dtypes


def mxq(x, axis, fmt="e4m3"):
    dtype, down = {"e4m3": (ml_dtypes.float8_e4m3fn, 7), "e5m2": (ml_dtypes.float8_e5m2, 14)}[fmt]
    v = np.moveaxis(np.asarray(x, np.float32).astype(ml_dtypes.bfloat16).astype(np.float64), axis, -1)
    blocks = v.reshape(v.shape[:-1] + (-1, 32))
    amax = np.abs(blocks).max(-1, keepdims=True)
    byte = np.maximum(np.where(amax > 0, np.frexp(amax)[1] - 1 + 127, 0) - down, 1)
    scale = np.exp2(byte - 127.0)
    codes = (blocks / scale).astype(np.float32).astype(dtype).astype(np.float64)
    return np.moveaxis((codes * scale).reshape(v.shape), -1, axis)


WIDE = False


def mx_kscale(k):
    if not WIDE:
        return np.ones(k)
    levels = np.array([10, -10, 5, -5, 0])
    if k % 512:
        return np.exp2(np.random.permutation(np.resize(levels, k // 32))).repeat(32)
    a = np.empty((k // 512, 16))
    for p in range(k // 512):
        a[p, :8] = np.random.permutation(np.resize(levels, 8))
        for g in range(8):
            far = levels[np.abs(levels - a[p, g]) >= 10]
            a[p, g + 8] = far[np.random.randint(len(far))]
    return np.exp2(a.ravel()).repeat(32)


BF16 = ml_dtypes.bfloat16


def bf(x):
    return np.asarray(x, np.float32).astype(BF16)


def f64(x):
    return np.asarray(x).astype(np.float64)


NB, S, DI, DO, R = 4, 128, 2048, 2048, 512
SCALE = 0.125


def setup_inputs():
    s, t = mx_kscale(R), mx_kscale(DI)
    return {"x": bf(np.random.standard_normal((NB, S, DI)) * t),
            "A": bf(np.random.standard_normal((R, DI)) * 3.0 / np.sqrt(DI) / s[:, None] / t),
            "B": bf(np.random.standard_normal((DO, R)) * 3.0 / np.sqrt(R) * s),
            "d_A": bf(1.0 + 0.1 * np.random.standard_normal(R)),
            "d_B": bf(np.random.standard_normal(DO))}


def reference(x, A, B, d_A, d_B):
    scaled_A = f64(d_A)[:, None] * f64(A)
    BA = mxq(f64(B), 1, "e4m3") @ mxq(scaled_A, 0, "e4m3")
    W = f64(d_B)[:, None] * BA
    return (mxq(f64(x), 2, "e4m3") @ mxq(W, 1, "e4m3").T) * SCALE

@@ -1,0 +1,227 @@
+from contextlib import ExitStack
+
+import concourse.mybir as mybir
+from concourse.masks import make_identity
+
+F32 = mybir.dt.float32
+BF16 = mybir.dt.bfloat16
+U32 = mybir.dt.uint32
+U8 = mybir.dt.uint8
+FP8X4 = mybir.dt.float8_e4m3fn_x4
+MULT = mybir.AluOpType.mult
+ADD = mybir.AluOpType.add
+COPY = mybir.ActivationFunctionType.Copy
+
+P = 128
+TOK, DI, DO, R = 512, 2048, 2048, 512
+CH = 512
+NG = DI // CH
+NOC = DO // CH
+N_UNITS = NOC * NG
+SCALE = 0.125
+LAG = 3
+G0 = 0
+FLOPS = 2 * DO * DI * R + 2 * TOK * DI * DO
+
+
+def tile_veralayer_pa_kernel(tc, x, A, B, d_A, d_B, out):
+    nc = tc.nc
+    with ExitStack() as ctx:
+        ctx.enter_context(tc.manual_schedule())
+        const = ctx.enter_context(tc.tile_pool(name="const", bufs=1))
+        raw = ctx.enter_context(tc.tile_pool(name="raw", bufs=1))
+        keep = ctx.enter_context(tc.tile_pool(name="keep", bufs=1))
+        grp = ctx.enter_context(tc.tile_pool(name="grp", bufs=4))
+        wgp = ctx.enter_context(tc.tile_pool(name="wgp", bufs=2))
+        outp = ctx.enter_context(tc.tile_pool(name="outp", bufs=6))
+        ps_w = ctx.enter_context(tc.psum_pool(name="ps_w", bufs=4))
+        ps_o = ctx.enter_context(tc.psum_pool(name="ps_o", bufs=1))
+
+        x_v = x.rearrange("b s i -> (b s) i").rearrange("(tt p) i -> p tt i", p=P)
+        out_v = out.rearrange("b s o -> (b s) o")
+        a_v = A.rearrange("(p t) i -> p t i", t=4)
+        b_v = B.rearrange("(ot p) r -> p ot r", p=P)
+
+        ident_f = const.tile([P, P], F32, name="ident_f")
+        da_b = const.tile([P, 4], BF16, name="da_b")
+        da_f = const.tile([P, 4], F32, name="da_f")
+        db_bc = [const.tile([P, CH], BF16, name="db_bc%d" % c) for c in range(NOC)]
+        a_raw = [raw.tile([P, 4, CH], BF16, name="a_raw%d" % g) for g in range(NG)]
+        x_raw = [raw.tile([P, 4 * CH], BF16, name="x_raw%d" % g) for g in range(NG)]
+        b_raw = [raw.tile([P, 4 * R], BF16, name="b_raw%d" % c) for c in range(NOC)]
+
+        def load(kind, k):
+            if kind == "a":
+                nc.sync.dma_start(out=a_raw[k][:], in_=a_v[:, :, k * CH : (k + 1) * CH])
+            elif kind == "x":
+                nc.sync.dma_start(
+                    out=x_raw[k][:].rearrange("p (tt i) -> p tt i", tt=4), in_=x_v[:, :, k * CH : (k + 1) * CH]
+                )
+            elif kind == "b":
+                nc.sync.dma_start(
+                    out=b_raw[k][:].rearrange("p (ot r) -> p ot r", ot=4), in_=b_v[:, 4 * k : 4 * k + 4, :]
+                )
+            else:
+                nc.sync.dma_start(out=db_bc[k][:], in_=d_B[k * CH : (k + 1) * CH].partition_broadcast(P))
+
+        nc.sync.dma_start(out=da_b[:], in_=d_A.rearrange("(p t) -> p t", t=4))
+        make_identity(nc, ident_f[:])
+        for kind, k in (("a", 0), ("b", 0), ("a", 1), ("d", 0), ("a", 2), ("x", 0), ("a", 3), ("x", 1), ("d", 1), ("b", 1), ("x", 2), ("x", 3), ("d", 2), ("b", 2), ("d", 3), ("b", 3)):
+            load(kind, k)
+        nc.vector.tensor_copy(out=da_f[:], in_=da_b[:])
+
+        codes = {}
+        for kind, count in (("a", NG), ("x", NG), ("b", NOC), ("w", N_UNITS)):
+            for k in range(count):
+                codes[(kind, k)] = (
+                    keep.tile([P, CH], U32, name="%s_c%d" % (kind, k), align_bytes=64),
+                    keep.tile([P, CH], U8, name="%s_s%d" % (kind, k), align_bytes=64),
+                )
+        grouped = {}
+        acc = {}
+
+        def words(kind, k, lo, hi):
+            return codes[(kind, k)][0][:, lo:hi].bitcast(FP8X4)
+
+        def scales(kind, k, lo, hi):
+            return codes[(kind, k)][1][:, lo:hi]
+
+        def copy_out(eng, dst, src):
+            if eng == "v":
+                nc.vector.tensor_copy(out=dst, in_=src)
+            else:
+                nc.scalar.copy(out=dst, in_=src)
+
+        def group_a(g, engs):
+            a_sc = grp.tile([P, 4, CH], BF16, name="a_sc", tag="a_sc")
+            for t in range(4):
+                nc.vector.tensor_scalar(
+                    out=a_sc[:, t, :], in0=a_raw[g][:, t, :], scalar1=da_f[:, t : t + 1], scalar2=0.0, op0=MULT, op1=ADD
+                )
+            ga = grp.tile([P, 4 * CH], BF16, name="ga", tag="grp", align_bytes=64)
+            grouped[("a", g)] = ga
+            for u in range(2):
+                copy_out(
+                    engs[u],
+                    ga[:, 2 * u * CH : 2 * (u + 1) * CH].rearrange("p (q m t) -> p q m t", q=2, t=4),
+                    a_sc[:].rearrange("p t (m q) -> p q m t", q=4)[:, 2 * u : 2 * u + 2],
+                )
+
+        def group_t(kind, k, engs):
+            src32 = (x_raw[k] if kind == "x" else b_raw[k])[:].bitcast(F32)
+            gk = grp.tile([P, 4 * CH], BF16, name="gk", tag="grp", align_bytes=64)
+            grouped[(kind, k)] = gk
+            gk32 = gk[:].bitcast(F32)
+            banks = [ps_w.tile([P, 2, 2, P], F32, name="bank_t", tag="w") for half in range(2)]
+            for half in range(2):
+                for j in range(2):
+                    for u in range(2):
+                        w0 = (2 * half + j) * 256
+                        nc.tensor.transpose(banks[half][:, j, u, :], src32[:, w0 + u : w0 + 256 : 2], ident_f[:])
+            for half in range(2):
+                copy_out(
+                    engs[half],
+                    gk32[:, half * CH : (half + 1) * CH].rearrange("p (j o u) -> p j o u", j=2, u=2),
+                    banks[half][:].rearrange("p j u o -> p j o u"),
+                )
+
+        def group(kind, k, engs):
+            if kind == "a":
+                group_a(k, engs)
+            else:
+                group_t(kind, k, engs)
+
+        def quantise(kind, k):
+            nc.vector.quantize_mx(out=words(kind, k, 0, CH), scales=scales(kind, k, 0, CH), in_=grouped[(kind, k)][:])
+
+        def w_banks(n, m):
+            oc, g = n // NG, n % NG
+            wgv = wgp.tile([P, 4 * CH], BF16, name="wgv", tag="wgv", align_bytes=64)
+            wgg = wgp.tile([P, CH], BF16, name="wgg", tag="wgg", bufs=1, align_bytes=64) if n >= G0 else None
+            grouped[("w", n)] = (wgv, wgg)
+            for ob in range(4):
+                bank = ps_w.tile([P, 4, P], F32, name="bank_w", tag="w")
+                for t in range(4):
+                    nc.tensor.matmul_mx(
+                        out=bank[:, t, :],
+                        lhsT=words("a", g, t * P, (t + 1) * P),
+                        lhsT_scale=scales("a", g, t * P, (t + 1) * P),
+                        rhs=words("b", oc, ob * P, (ob + 1) * P),
+                        rhs_scale=scales("b", oc, ob * P, (ob + 1) * P),
+                        start=True,
+                        stop=True,
+                    )
+                if m is not None:
+                    second_pass(m, ob)
+                db = db_bc[oc][:, ob * P : (ob + 1) * P].unsqueeze(2).to_broadcast([P, P, 4])
+                if ob == 0 and n >= G0:
+                    wf = wgp.tile([P, CH], F32, name="wf", tag="wf")
+                    nc.scalar.copy(out=wf[:].rearrange("p (o t) -> p o t", t=4), in_=bank[:].rearrange("p t o -> p o t"))
+                    nc.gpsimd.tensor_tensor(
+                        out=wgg[:].rearrange("p (o t) -> p o t", t=4),
+                        in0=wf[:].rearrange("p (o t) -> p o t", t=4),
+                        in1=db,
+                        op=MULT,
+                    )
+                else:
+                    nc.vector.tensor_tensor(
+                        out=wgv[:, ob * CH : (ob + 1) * CH].rearrange("p (o t) -> p o t", t=4),
+                        in0=bank[:].rearrange("p t o -> p o t"),
+                        in1=db,
+                        op=MULT,
+                    )
+
+        def w_quantise(n):
+            wgv, wgg = grouped[("w", n)]
+            if n < G0:
+                nc.vector.quantize_mx(out=words("w", n, 0, CH), scales=scales("w", n, 0, CH), in_=wgv[:])
+                return
+            for lo, hi, src in ((P, 3 * P, wgv[:, CH : 3 * CH]), (3 * P, 4 * P, wgv[:, 3 * CH : 4 * CH]), (0, P, wgg[:])):
+                nc.vector.quantize_mx(out=words("w", n, lo, hi), scales=scales("w", n, lo, hi), in_=src)
+
+        def second_pass(n, tt):
+            oc, g = n // NG, n % NG
+            if g == 0:
+                acc[tt] = ps_o.tile([P, CH], F32, name="acc%d" % tt, tag="acc%d" % tt)
+            nc.tensor.matmul_mx(
+                out=acc[tt][:],
+                lhsT=words("x", g, tt * P, (tt + 1) * P),
+                lhsT_scale=scales("x", g, tt * P, (tt + 1) * P),
+                rhs=words("w", n, 0, CH),
+                rhs_scale=scales("w", n, 0, CH),
+                start=(g == 0),
+                stop=(g == NG - 1),
+            )
+
+        def store_out(oc, engs):
+            for tt in range(4):
+                o_sb = outp.tile([P, CH], F32, name="o_sb", tag="o_sb")
+                if engs[tt] == "v":
+                    nc.vector.tensor_scalar_mul(out=o_sb[:], in0=acc[tt][:], scalar1=SCALE)
+                else:
+                    nc.scalar.activation(out=o_sb[:], in_=acc[tt][:], func=COPY, scale=SCALE)
+                nc.sync.dma_start(out=out_v[tt * P : (tt + 1) * P, oc * CH : (oc + 1) * CH], in_=o_sb[:])
+
+        group("a", 0, "vs")
+        group("b", 0, "vs")
+        quantise("a", 0)
+        quantise("b", 0)
+        pending = [("a", 1), ("a", 2)]
+        for kind, k in pending:
+            group(kind, k, "vs" if kind == "a" else "ss")
+        later = {0: [("x", 0), ("a", 3)], 1: [("x", 1), ("b", 1)], 2: [("x", 2)], 3: [("x", 3)], 5: [("b", 2)], 9: [("b", 3)]}
+        for n in range(N_UNITS):
+            m = n - LAG if n >= LAG else None
+            w_banks(n, m)
+            for kind, k in pending:
+                quantise(kind, k)
+            w_quantise(n)
+            if m is not None and m % NG == NG - 1:
+                store_out(m // NG, "ssss")
+            pending = later.get(n, [])
+            for kind, k in pending:
+                group(kind, k, "vs" if kind == "a" else "ss")
+        for m in range(N_UNITS - LAG, N_UNITS):
+            for tt in range(4):
+                second_pass(m, tt)
+        store_out(NOC - 1, "svsv")

@@ -20,7 +20,6 @@ NOC = DO // CH
 N_UNITS = NOC * NG
 SCALE = 0.125
 LAG = 3
-G0 = 0
 FLOPS = 2 * DO * DI * R + 2 * TOK * DI * DO
 
 
@@ -66,7 +65,7 @@ def tile_veralayer_pa_kernel(tc, x, A, B, d_A, d_B, out):
 
         nc.sync.dma_start(out=da_b[:], in_=d_A.rearrange("(p t) -> p t", t=4))
         make_identity(nc, ident_f[:])
-        for kind, k in (("a", 0), ("b", 0), ("a", 1), ("d", 0), ("a", 2), ("x", 0), ("a", 3), ("x", 1), ("d", 1), ("b", 1), ("x", 2), ("x", 3), ("d", 2), ("b", 2), ("d", 3), ("b", 3)):
+        for kind, k in (("a", 0), ("b", 0), ("a", 1), ("d", 0), ("a", 2), ("x", 0), ("a", 3), ("b", 1), ("x", 1), ("d", 1), ("x", 2), ("b", 2), ("x", 3), ("d", 2), ("b", 3), ("d", 3)):
             load(kind, k)
         nc.vector.tensor_copy(out=da_f[:], in_=da_b[:])
 
@@ -77,6 +76,7 @@ def tile_veralayer_pa_kernel(tc, x, A, B, d_A, d_B, out):
                     keep.tile([P, CH], U32, name="%s_c%d" % (kind, k), align_bytes=64),
                     keep.tile([P, CH], U8, name="%s_s%d" % (kind, k), align_bytes=64),
                 )
+        scaled = {}
         grouped = {}
         acc = {}
 
@@ -92,90 +92,84 @@ def tile_veralayer_pa_kernel(tc, x, A, B, d_A, d_B, out):
             else:
                 nc.scalar.copy(out=dst, in_=src)
 
-        def group_a(g, engs):
+        def scale_a(g):
             a_sc = grp.tile([P, 4, CH], BF16, name="a_sc", tag="a_sc")
+            scaled[g] = a_sc
             for t in range(4):
                 nc.vector.tensor_scalar(
                     out=a_sc[:, t, :], in0=a_raw[g][:, t, :], scalar1=da_f[:, t : t + 1], scalar2=0.0, op0=MULT, op1=ADD
                 )
-            ga = grp.tile([P, 4 * CH], BF16, name="ga", tag="grp", align_bytes=64)
-            grouped[("a", g)] = ga
-            for u in range(2):
-                copy_out(
-                    engs[u],
-                    ga[:, 2 * u * CH : 2 * (u + 1) * CH].rearrange("p (q m t) -> p q m t", q=2, t=4),
-                    a_sc[:].rearrange("p t (m q) -> p q m t", q=4)[:, 2 * u : 2 * u + 2],
-                )
 
-        def group_t(kind, k, engs):
+        def regroup_a(g, q0, q1, eng):
+            if ("a", g) not in grouped:
+                ga = grp.tile([P, 4 * CH], BF16, name="ga", tag="grp", align_bytes=64)
+                grouped[("a", g)] = ga
+            copy_out(
+                eng,
+                grouped[("a", g)][:, q0 * CH : q1 * CH].rearrange("p (q m t) -> p q m t", q=q1 - q0, t=4),
+                scaled[g][:].rearrange("p t (m q) -> p q m t", q=4)[:, q0:q1],
+            )
+
+        def transpose_half(kind, k, half, eng):
             src32 = (x_raw[k] if kind == "x" else b_raw[k])[:].bitcast(F32)
-            gk = grp.tile([P, 4 * CH], BF16, name="gk", tag="grp", align_bytes=64)
-            grouped[(kind, k)] = gk
-            gk32 = gk[:].bitcast(F32)
-            banks = [ps_w.tile([P, 2, 2, P], F32, name="bank_t", tag="w") for half in range(2)]
-            for half in range(2):
-                for j in range(2):
-                    for u in range(2):
-                        w0 = (2 * half + j) * 256
-                        nc.tensor.transpose(banks[half][:, j, u, :], src32[:, w0 + u : w0 + 256 : 2], ident_f[:])
-            for half in range(2):
-                copy_out(
-                    engs[half],
-                    gk32[:, half * CH : (half + 1) * CH].rearrange("p (j o u) -> p j o u", j=2, u=2),
-                    banks[half][:].rearrange("p j u o -> p j o u"),
-                )
-
-        def group(kind, k, engs):
-            if kind == "a":
-                group_a(k, engs)
-            else:
-                group_t(kind, k, engs)
+            if (kind, k) not in grouped:
+                gk = grp.tile([P, 4 * CH], BF16, name="gk", tag="grp", align_bytes=64)
+                grouped[(kind, k)] = gk
+            gk32 = grouped[(kind, k)][:].bitcast(F32)
+            bank = ps_w.tile([P, 2, 2, P], F32, name="bank_t", tag="w")
+            for j in range(2):
+                for u in range(2):
+                    w0 = (2 * half + j) * 256
+                    nc.tensor.transpose(bank[:, j, u, :], src32[:, w0 + u : w0 + 256 : 2], ident_f[:])
+            copy_out(
+                eng,
+                gk32[:, half * CH : (half + 1) * CH].rearrange("p (j o u) -> p j o u", j=2, u=2),
+                bank[:].rearrange("p j u o -> p j o u"),
+            )
 
         def quantise(kind, k):
             nc.vector.quantize_mx(out=words(kind, k, 0, CH), scales=scales(kind, k, 0, CH), in_=grouped[(kind, k)][:])
 
-        def w_banks(n, m):
+        def w_bank(n, ob, m):
             oc, g = n // NG, n % NG
-            wgv = wgp.tile([P, 4 * CH], BF16, name="wgv", tag="wgv", align_bytes=64)
-            wgg = wgp.tile([P, CH], BF16, name="wgg", tag="wgg", bufs=1, align_bytes=64) if n >= G0 else None
-            grouped[("w", n)] = (wgv, wgg)
-            for ob in range(4):
-                bank = ps_w.tile([P, 4, P], F32, name="bank_w", tag="w")
-                for t in range(4):
-                    nc.tensor.matmul_mx(
-                        out=bank[:, t, :],
-                        lhsT=words("a", g, t * P, (t + 1) * P),
-                        lhsT_scale=scales("a", g, t * P, (t + 1) * P),
-                        rhs=words("b", oc, ob * P, (ob + 1) * P),
-                        rhs_scale=scales("b", oc, ob * P, (ob + 1) * P),
-                        start=True,
-                        stop=True,
-                    )
-                if m is not None:
-                    second_pass(m, ob)
-                db = db_bc[oc][:, ob * P : (ob + 1) * P].unsqueeze(2).to_broadcast([P, P, 4])
-                if ob == 0 and n >= G0:
-                    wf = wgp.tile([P, CH], F32, name="wf", tag="wf")
-                    nc.scalar.copy(out=wf[:].rearrange("p (o t) -> p o t", t=4), in_=bank[:].rearrange("p t o -> p o t"))
-                    nc.gpsimd.tensor_tensor(
-                        out=wgg[:].rearrange("p (o t) -> p o t", t=4),
-                        in0=wf[:].rearrange("p (o t) -> p o t", t=4),
-                        in1=db,
-                        op=MULT,
-                    )
-                else:
-                    nc.vector.tensor_tensor(
-                        out=wgv[:, ob * CH : (ob + 1) * CH].rearrange("p (o t) -> p o t", t=4),
-                        in0=bank[:].rearrange("p t o -> p o t"),
-                        in1=db,
-                        op=MULT,
-                    )
+            if ob == 0:
+                wgv = wgp.tile([P, 4 * CH], BF16, name="wgv", tag="wgv", align_bytes=64)
+                wgg = wgp.tile([P, CH], BF16, name="wgg", tag="wgg", bufs=1, align_bytes=64)
+                grouped[("w", n)] = (wgv, wgg)
+            wgv, wgg = grouped[("w", n)]
+            bank = ps_w.tile([P, 4, P], F32, name="bank_w", tag="w")
+            for t in range(4):
+                nc.tensor.matmul_mx(
+                    out=bank[:, t, :],
+                    lhsT=words("a", g, t * P, (t + 1) * P),
+                    lhsT_scale=scales("a", g, t * P, (t + 1) * P),
+                    rhs=words("b", oc, ob * P, (ob + 1) * P),
+                    rhs_scale=scales("b", oc, ob * P, (ob + 1) * P),
+                    start=True,
+                    stop=True,
+                )
+            if m is not None:
+                second_pass(m, ob)
+            db = db_bc[oc][:, ob * P : (ob + 1) * P].unsqueeze(2).to_broadcast([P, P, 4])
+            if ob == 0:
+                wf = wgp.tile([P, CH], F32, name="wf", tag="wf")
+                nc.scalar.copy(out=wf[:].rearrange("p (o t) -> p o t", t=4), in_=bank[:].rearrange("p t o -> p o t"))
+                nc.gpsimd.tensor_tensor(
+                    out=wgg[:].rearrange("p (o t) -> p o t", t=4),
+                    in0=wf[:].rearrange("p (o t) -> p o t", t=4),
+                    in1=db,
+                    op=MULT,
+                )
+            else:
+                nc.vector.tensor_tensor(
+                    out=wgv[:, ob * CH : (ob + 1) * CH].rearrange("p (o t) -> p o t", t=4),
+                    in0=bank[:].rearrange("p t o -> p o t"),
+                    in1=db,
+                    op=MULT,
+                )
 
         def w_quantise(n):
             wgv, wgg = grouped[("w", n)]
-            if n < G0:
-                nc.vector.quantize_mx(out=words("w", n, 0, CH), scales=scales("w", n, 0, CH), in_=wgv[:])
-                return
             for lo, hi, src in ((P, 3 * P, wgv[:, CH : 3 * CH]), (3 * P, 4 * P, wgv[:, 3 * CH : 4 * CH]), (0, P, wgg[:])):
                 nc.vector.quantize_mx(out=words("w", n, lo, hi), scales=scales("w", n, lo, hi), in_=src)
 
@@ -202,25 +196,37 @@ def tile_veralayer_pa_kernel(tc, x, A, B, d_A, d_B, out):
                     nc.scalar.activation(out=o_sb[:], in_=acc[tt][:], func=COPY, scale=SCALE)
                 nc.sync.dma_start(out=out_v[tt * P : (tt + 1) * P, oc * CH : (oc + 1) * CH], in_=o_sb[:])
 
-        group("a", 0, "vs")
-        group("b", 0, "vs")
+        scale_a(0)
+        regroup_a(0, 0, 3, "v")
+        regroup_a(0, 3, 4, "s")
+        for half in range(2):
+            transpose_half("b", 0, half, "s")
         quantise("a", 0)
         quantise("b", 0)
-        pending = [("a", 1), ("a", 2)]
-        for kind, k in pending:
-            group(kind, k, "vs" if kind == "a" else "ss")
-        later = {0: [("x", 0), ("a", 3)], 1: [("x", 1), ("b", 1)], 2: [("x", 2)], 3: [("x", 3)], 5: [("b", 2)], 9: [("b", 3)]}
+        scale_a(1)
         for n in range(N_UNITS):
             m = n - LAG if n >= LAG else None
-            w_banks(n, m)
-            for kind, k in pending:
-                quantise(kind, k)
+            for ob in range(4):
+                w_bank(n, ob, m)
+                if n + 1 < NG:
+                    regroup_a(n + 1, ob, ob + 1, "v" if ob == 3 else "s")
+            if n + 2 < NG:
+                scale_a(n + 2)
+            if n < 4:
+                for kind in ("x", "b"):
+                    k = n if kind == "x" else n + 1
+                    if k < 4:
+                        for half in range(2):
+                            transpose_half(kind, k, half, "s")
+            if n + 1 < NG:
+                quantise("a", n + 1)
             w_quantise(n)
+            if n < 4:
+                quantise("x", n)
+                if n < 3:
+                    quantise("b", n + 1)
             if m is not None and m % NG == NG - 1:
                 store_out(m // NG, "ssss")
-            pending = later.get(n, [])
-            for kind, k in pending:
-                group(kind, k, "vs" if kind == "a" else "ss")
         for m in range(N_UNITS - LAG, N_UNITS):
             for tt in range(4):
                 second_pass(m, tt)

@@ -6,6 +6,7 @@ from concourse.masks import make_identity
 F32 = mybir.dt.float32
 BF16 = mybir.dt.bfloat16
 U32 = mybir.dt.uint32
+I32 = mybir.dt.int32
 U8 = mybir.dt.uint8
 FP8X4 = mybir.dt.float8_e4m3fn_x4
 MULT = mybir.AluOpType.mult
@@ -38,34 +39,35 @@ def tile_veralayer_pa_kernel(tc, x, A, B, d_A, d_B, out):
 
         x_v = x.rearrange("b s i -> (b s) i").rearrange("(tt p) i -> p tt i", p=P)
         out_v = out.rearrange("b s o -> (b s) o")
+        d_row = d_B.unsqueeze(0)
         a_v = A.rearrange("(p t) i -> p t i", t=4)
-        b_v = B.rearrange("(ot p) r -> p ot r", p=P)
+        b_v = B.rearrange("(c p j) r -> c p (j r)", p=P, j=4)
 
         ident_f = const.tile([P, P], F32, name="ident_f")
         da_b = const.tile([P, 4], BF16, name="da_b")
         da_f = const.tile([P, 4], F32, name="da_f")
+        ones = const.tile([P, P], BF16, name="ones")
+        db_row = const.tile([P, DO], BF16, name="db_row")
         db_bc = [const.tile([P, CH], BF16, name="db_bc%d" % c) for c in range(NOC)]
         a_raw = [raw.tile([P, 4, CH], BF16, name="a_raw%d" % g) for g in range(NG)]
-        x_raw = [raw.tile([P, 4 * CH], BF16, name="x_raw%d" % g) for g in range(NG)]
+        x_raw = [raw.tile([P, 4, 2 * CH], BF16, name="x_raw%d" % h) for h in range(2)]
         b_raw = [raw.tile([P, 4 * R], BF16, name="b_raw%d" % c) for c in range(NOC)]
 
         def load(kind, k):
             if kind == "a":
                 nc.sync.dma_start(out=a_raw[k][:], in_=a_v[:, :, k * CH : (k + 1) * CH])
             elif kind == "x":
-                nc.sync.dma_start(
-                    out=x_raw[k][:].rearrange("p (tt i) -> p tt i", tt=4), in_=x_v[:, :, k * CH : (k + 1) * CH]
-                )
+                nc.sync.dma_start(out=x_raw[k][:], in_=x_v[:, :, 2 * k * CH : 2 * (k + 1) * CH])
             elif kind == "b":
-                nc.sync.dma_start(
-                    out=b_raw[k][:].rearrange("p (ot r) -> p ot r", ot=4), in_=b_v[:, 4 * k : 4 * k + 4, :]
-                )
+                nc.sync.dma_start(out=b_raw[k][:], in_=b_v[k])
             else:
-                nc.sync.dma_start(out=db_bc[k][:], in_=d_B[k * CH : (k + 1) * CH].partition_broadcast(P))
+                nc.sync.dma_start(out=db_row[0:1, :], in_=d_row)
 
         nc.sync.dma_start(out=da_b[:], in_=d_A.rearrange("(p t) -> p t", t=4))
+        nc.vector.memset(db_row[:].bitcast(I32), 0)
+        nc.vector.memset(ones[:], 1.0)
         make_identity(nc, ident_f[:])
-        for kind, k in (("a", 0), ("b", 0), ("a", 1), ("d", 0), ("a", 2), ("x", 0), ("a", 3), ("b", 1), ("x", 1), ("d", 1), ("x", 2), ("b", 2), ("x", 3), ("d", 2), ("b", 3), ("d", 3)):
+        for kind, k in (("d", 0), ("a", 0), ("b", 0), ("a", 1), ("a", 2), ("x", 0), ("a", 3), ("b", 1), ("x", 1), ("b", 2), ("b", 3)):
             load(kind, k)
         nc.vector.tensor_copy(out=da_f[:], in_=da_b[:])
 
@@ -111,7 +113,12 @@ def tile_veralayer_pa_kernel(tc, x, A, B, d_A, d_B, out):
             )
 
         def transpose_half(kind, k, half, eng):
-            src32 = (x_raw[k] if kind == "x" else b_raw[k])[:].bitcast(F32)
+            if kind == "x":
+                src = x_raw[k // 2][:].rearrange("p tt i -> p (tt i)").bitcast(F32)
+                row, w0 = CH, (k % 2) * (CH // 2)
+            else:
+                src = b_raw[k][:].bitcast(F32)
+                row, w0 = CH // 2, 0
             if (kind, k) not in grouped:
                 gk = grp.tile([P, 4 * CH], BF16, name="gk", tag="grp", align_bytes=64)
                 grouped[(kind, k)] = gk
@@ -119,8 +126,8 @@ def tile_veralayer_pa_kernel(tc, x, A, B, d_A, d_B, out):
             bank = ps_w.tile([P, 2, 2, P], F32, name="bank_t", tag="w")
             for j in range(2):
                 for u in range(2):
-                    w0 = (2 * half + j) * 256
-                    nc.tensor.transpose(bank[:, j, u, :], src32[:, w0 + u : w0 + 256 : 2], ident_f[:])
+                    w = (2 * half + j) * row + w0
+                    nc.tensor.transpose(bank[:, j, u, :], src[:, w + u : w + CH // 2 : 2], ident_f[:])
             copy_out(
                 eng,
                 gk32[:, half * CH : (half + 1) * CH].rearrange("p (j o u) -> p j o u", j=2, u=2),
@@ -129,6 +136,13 @@ def tile_veralayer_pa_kernel(tc, x, A, B, d_A, d_B, out):
 
         def quantise(kind, k):
             nc.vector.quantize_mx(out=words(kind, k, 0, CH), scales=scales(kind, k, 0, CH), in_=grouped[(kind, k)][:])
+
+        def quantise_half(kind, k, h):
+            nc.vector.quantize_mx(
+                out=words(kind, k, 256 * h, 256 * (h + 1)),
+                scales=scales(kind, k, 256 * h, 256 * (h + 1)),
+                in_=grouped[(kind, k)][:, 1024 * h : 1024 * (h + 1)],
+            )
 
         def w_bank(n, ob, m):
             oc, g = n // NG, n % NG
@@ -168,6 +182,14 @@ def tile_veralayer_pa_kernel(tc, x, A, B, d_A, d_B, out):
                     op=MULT,
                 )
 
+        def spread_d_b():
+            for c in range(NOC):
+                bank = ps_o.tile([P, CH], F32, name="bank_d", tag="acc%d" % c)
+                nc.tensor.matmul(out=bank[:], lhsT=ones[:], rhs=db_row[:, c * CH : (c + 1) * CH], start=True, stop=True)
+                nc.scalar.copy(
+                    out=db_bc[c][:].rearrange("p (j o) -> p j o", j=4), in_=bank[:].rearrange("p (o j) -> p j o", j=4)
+                )
+
         def w_quantise(n):
             wgv, wgg = grouped[("w", n)]
             for lo, hi, src in ((P, 3 * P, wgv[:, CH : 3 * CH]), (3 * P, 4 * P, wgv[:, 3 * CH : 4 * CH]), (0, P, wgg[:])):
@@ -191,18 +213,20 @@ def tile_veralayer_pa_kernel(tc, x, A, B, d_A, d_B, out):
             for tt in range(4):
                 o_sb = outp.tile([P, CH], F32, name="o_sb", tag="o_sb")
                 if engs[tt] == "v":
-                    nc.vector.tensor_scalar_mul(out=o_sb[:], in0=acc[tt][:], scalar1=SCALE)
+                    nc.vector.tensor_scalar_mul(out=o_sb[:].rearrange("p (o j) -> p o j", j=4), in0=acc[tt][:].rearrange("p (j o) -> p o j", j=4), scalar1=SCALE)
                 else:
-                    nc.scalar.activation(out=o_sb[:], in_=acc[tt][:], func=COPY, scale=SCALE)
+                    nc.scalar.activation(out=o_sb[:].rearrange("p (o j) -> p o j", j=4), in_=acc[tt][:].rearrange("p (j o) -> p o j", j=4), func=COPY, scale=SCALE)
                 nc.sync.dma_start(out=out_v[tt * P : (tt + 1) * P, oc * CH : (oc + 1) * CH], in_=o_sb[:])
 
+        spread_d_b()
         scale_a(0)
         regroup_a(0, 0, 3, "v")
         regroup_a(0, 3, 4, "s")
         for half in range(2):
             transpose_half("b", 0, half, "s")
         quantise("a", 0)
-        quantise("b", 0)
+        quantise_half("b", 0, 0)
+        quantise_half("b", 0, 1)
         scale_a(1)
         for n in range(N_UNITS):
             m = n - LAG if n >= LAG else None

@@ -54,7 +54,9 @@ def tile_veralayer_pa_kernel(tc, x, A, B, d_A, d_B, out):
         b_raw = [raw.tile([P, 4 * R], BF16, name="b_raw%d" % c) for c in range(NOC)]
 
         def load(kind, k):
-            if kind == "a":
+            if kind == "da":
+                nc.sync.dma_start(out=da_b[:], in_=d_A.rearrange("(p t) -> p t", t=4))
+            elif kind == "a":
                 nc.sync.dma_start(out=a_raw[k][:], in_=a_v[:, :, k * CH : (k + 1) * CH])
             elif kind == "x":
                 nc.sync.dma_start(out=x_raw[k][:], in_=x_v[:, :, 2 * k * CH : 2 * (k + 1) * CH])
@@ -63,11 +65,10 @@ def tile_veralayer_pa_kernel(tc, x, A, B, d_A, d_B, out):
             else:
                 nc.sync.dma_start(out=db_row[0:1, :], in_=d_row)
 
-        nc.sync.dma_start(out=da_b[:], in_=d_A.rearrange("(p t) -> p t", t=4))
         nc.vector.memset(db_row[:].bitcast(I32), 0)
         nc.vector.memset(ones[:], 1.0)
         make_identity(nc, ident_f[:])
-        for kind, k in (("d", 0), ("a", 0), ("b", 0), ("a", 1), ("a", 2), ("x", 0), ("a", 3), ("b", 1), ("x", 1), ("b", 2), ("b", 3)):
+        for kind, k in (("a", 0), ("da", 0), ("d", 0), ("b", 0), ("a", 1), ("a", 2), ("x", 0), ("a", 3), ("b", 1), ("x", 1), ("b", 2), ("b", 3)):
             load(kind, k)
         nc.vector.tensor_copy(out=da_f[:], in_=da_b[:])
 
@@ -102,14 +103,14 @@ def tile_veralayer_pa_kernel(tc, x, A, B, d_A, d_B, out):
                     out=a_sc[:, t, :], in0=a_raw[g][:, t, :], scalar1=da_f[:, t : t + 1], scalar2=0.0, op0=MULT, op1=ADD
                 )
 
-        def regroup_a(g, q0, q1, eng):
+        def regroup_a(g, r0, r1, eng):
             if ("a", g) not in grouped:
                 ga = grp.tile([P, 4 * CH], BF16, name="ga", tag="grp", align_bytes=64)
                 grouped[("a", g)] = ga
             copy_out(
                 eng,
-                grouped[("a", g)][:, q0 * CH : q1 * CH].rearrange("p (q m t) -> p q m t", q=q1 - q0, t=4),
-                scaled[g][:].rearrange("p t (m q) -> p q m t", q=4)[:, q0:q1],
+                grouped[("a", g)][:].rearrange("p (q m t) -> p m t q", q=4, t=4)[:, r0 * 32 : r1 * 32],
+                scaled[g][:].rearrange("p t (m q) -> p m t q", q=4)[:, r0 * 32 : r1 * 32],
             )
 
         def transpose_half(kind, k, half, eng):
@@ -218,12 +219,12 @@ def tile_veralayer_pa_kernel(tc, x, A, B, d_A, d_B, out):
                     nc.scalar.activation(out=o_sb[:].rearrange("p (o j) -> p o j", j=4), in_=acc[tt][:].rearrange("p (j o) -> p o j", j=4), func=COPY, scale=SCALE)
                 nc.sync.dma_start(out=out_v[tt * P : (tt + 1) * P, oc * CH : (oc + 1) * CH], in_=o_sb[:])
 
-        spread_d_b()
         scale_a(0)
         regroup_a(0, 0, 3, "v")
         regroup_a(0, 3, 4, "s")
         for half in range(2):
             transpose_half("b", 0, half, "s")
+        spread_d_b()
         quantise("a", 0)
         quantise_half("b", 0, 0)
         quantise_half("b", 0, 1)

@@ -20,7 +20,7 @@ NG = DI // CH
 NOC = DO // CH
 N_UNITS = NOC * NG
 SCALE = 0.125
-LAG = 3
+LAG = 2
 FLOPS = 2 * DO * DI * R + 2 * TOK * DI * DO
 
 
@@ -68,7 +68,7 @@ def tile_veralayer_pa_kernel(tc, x, A, B, d_A, d_B, out):
         nc.vector.memset(db_row[:].bitcast(I32), 0)
         nc.vector.memset(ones[:], 1.0)
         make_identity(nc, ident_f[:])
-        for kind, k in (("a", 0), ("da", 0), ("d", 0), ("b", 0), ("a", 1), ("a", 2), ("x", 0), ("a", 3), ("b", 1), ("x", 1), ("b", 2), ("b", 3)):
+        for kind, k in (("a", 0), ("da", 0), ("d", 0), ("b", 0), ("a", 1), ("x", 0), ("a", 2), ("x", 1), ("a", 3), ("b", 1), ("b", 2), ("b", 3)):
             load(kind, k)
         nc.vector.tensor_copy(out=da_f[:], in_=da_b[:])
 
@@ -229,27 +229,23 @@ def tile_veralayer_pa_kernel(tc, x, A, B, d_A, d_B, out):
         quantise_half("b", 0, 0)
         quantise_half("b", 0, 1)
         scale_a(1)
+        prepare = {0: [("x", 0), ("x", 1)], 1: [("x", 2), ("x", 3)], 2: [("b", 1), ("b", 2)], 3: [("b", 3)]}
         for n in range(N_UNITS):
             m = n - LAG if n >= LAG else None
             for ob in range(4):
                 w_bank(n, ob, m)
                 if n + 1 < NG:
-                    regroup_a(n + 1, ob, ob + 1, "v" if ob == 3 else "s")
+                    regroup_a(n + 1, ob, ob + 1, "s")
             if n + 2 < NG:
                 scale_a(n + 2)
-            if n < 4:
-                for kind in ("x", "b"):
-                    k = n if kind == "x" else n + 1
-                    if k < 4:
-                        for half in range(2):
-                            transpose_half(kind, k, half, "s")
+            for kind, k in prepare.get(n, []):
+                for half in range(2):
+                    transpose_half(kind, k, half, "s")
             if n + 1 < NG:
                 quantise("a", n + 1)
             w_quantise(n)
-            if n < 4:
-                quantise("x", n)
-                if n < 3:
-                    quantise("b", n + 1)
+            for kind, k in prepare.get(n, []):
+                quantise(kind, k)
             if m is not None and m % NG == NG - 1:
                 store_out(m // NG, "ssss")
         for m in range(N_UNITS - LAG, N_UNITS):

@@ -39,7 +39,6 @@ def tile_veralayer_pa_kernel(tc, x, A, B, d_A, d_B, out):
 
         x_v = x.rearrange("b s i -> (b s) i").rearrange("(tt p) i -> p tt i", p=P)
         out_v = out.rearrange("b s o -> (b s) o")
-        d_row = d_B.unsqueeze(0)
         a_v = A.rearrange("(p t) i -> p t i", t=4)
         b_v = B.rearrange("(c p j) r -> c p (j r)", p=P, j=4)
 
@@ -47,8 +46,9 @@ def tile_veralayer_pa_kernel(tc, x, A, B, d_A, d_B, out):
         da_b = const.tile([P, 4], BF16, name="da_b")
         da_f = const.tile([P, 4], F32, name="da_f")
         ones = const.tile([P, P], BF16, name="ones")
-        db_row = const.tile([P, DO], BF16, name="db_row")
-        db_bc = [const.tile([P, CH], BF16, name="db_bc%d" % c) for c in range(NOC)]
+        db_row = const.tile([P, CH], BF16, name="db_row")
+        db_first = const.tile([P, CH], BF16, name="db_first")
+        db_rest = const.tile([P, DO - CH], BF16, name="db_rest")
         a_raw = [raw.tile([P, 4, CH], BF16, name="a_raw%d" % g) for g in range(NG)]
         x_raw = [raw.tile([P, 4, 2 * CH], BF16, name="x_raw%d" % h) for h in range(2)]
         b_raw = [raw.tile([P, 4 * R], BF16, name="b_raw%d" % c) for c in range(NOC)]
@@ -63,13 +63,14 @@ def tile_veralayer_pa_kernel(tc, x, A, B, d_A, d_B, out):
             elif kind == "b":
                 nc.sync.dma_start(out=b_raw[k][:], in_=b_v[k])
             else:
-                nc.sync.dma_start(out=db_row[0:1, :], in_=d_row)
+                nc.sync.dma_start(out=db_row[0:1, :], in_=d_B[0:CH].unsqueeze(0))
 
         nc.vector.memset(db_row[:].bitcast(I32), 0)
         nc.vector.memset(ones[:], 1.0)
         make_identity(nc, ident_f[:])
         for kind, k in (("a", 0), ("da", 0), ("d", 0), ("b", 0), ("a", 1), ("x", 0), ("a", 2), ("x", 1), ("a", 3), ("b", 1), ("b", 2), ("b", 3)):
             load(kind, k)
+        nc.sync.dma_start(out=db_rest[:], in_=d_B[CH:DO].partition_broadcast(P))
         nc.vector.tensor_copy(out=da_f[:], in_=da_b[:])
 
         codes = {}
@@ -165,7 +166,8 @@ def tile_veralayer_pa_kernel(tc, x, A, B, d_A, d_B, out):
                 )
             if m is not None:
                 second_pass(m, ob)
-            db = db_bc[oc][:, ob * P : (ob + 1) * P].unsqueeze(2).to_broadcast([P, P, 4])
+            db_chunk = db_first[:] if oc == 0 else db_rest[:, (oc - 1) * CH : oc * CH]
+            db = db_chunk.rearrange("p (o j) -> p j o", j=4)[:, ob].unsqueeze(2).to_broadcast([P, P, 4])
             if ob == 0:
                 wf = wgp.tile([P, CH], F32, name="wf", tag="wf")
                 nc.scalar.copy(out=wf[:].rearrange("p (o t) -> p o t", t=4), in_=bank[:].rearrange("p t o -> p o t"))
@@ -184,12 +186,9 @@ def tile_veralayer_pa_kernel(tc, x, A, B, d_A, d_B, out):
                 )
 
         def spread_d_b():
-            for c in range(NOC):
-                bank = ps_o.tile([P, CH], F32, name="bank_d", tag="acc%d" % c)
-                nc.tensor.matmul(out=bank[:], lhsT=ones[:], rhs=db_row[:, c * CH : (c + 1) * CH], start=True, stop=True)
-                nc.scalar.copy(
-                    out=db_bc[c][:].rearrange("p (j o) -> p j o", j=4), in_=bank[:].rearrange("p (o j) -> p j o", j=4)
-                )
+            bank = ps_o.tile([P, CH], F32, name="bank_d", tag="acc0")
+            nc.tensor.matmul(out=bank[:], lhsT=ones[:], rhs=db_row[:], start=True, stop=True)
+            nc.scalar.copy(out=db_first[:], in_=bank[:])
 
         def w_quantise(n):
             wgv, wgg = grouped[("w", n)]
@@ -229,21 +228,22 @@ def tile_veralayer_pa_kernel(tc, x, A, B, d_A, d_B, out):
         quantise_half("b", 0, 0)
         quantise_half("b", 0, 1)
         scale_a(1)
+        regroup_a(1, 0, 2, "v")
         prepare = {0: [("x", 0), ("x", 1)], 1: [("x", 2), ("x", 3)], 2: [("b", 1), ("b", 2)], 3: [("b", 3)]}
         for n in range(N_UNITS):
             m = n - LAG if n >= LAG else None
             for ob in range(4):
                 w_bank(n, ob, m)
-                if n + 1 < NG:
+                if n + 1 < NG and (n > 0 or ob >= 2):
                     regroup_a(n + 1, ob, ob + 1, "s")
-            if n + 2 < NG:
-                scale_a(n + 2)
             for kind, k in prepare.get(n, []):
                 for half in range(2):
                     transpose_half(kind, k, half, "s")
             if n + 1 < NG:
                 quantise("a", n + 1)
             w_quantise(n)
+            if n + 2 < NG:
+                scale_a(n + 2)
             for kind, k in prepare.get(n, []):
                 quantise(kind, k)
             if m is not None and m % NG == NG - 1:

@@ -18,9 +18,10 @@ TOK, DI, DO, R = 512, 2048, 2048, 512
 CH = 512
 NG = DI // CH
 NOC = DO // CH
-N_UNITS = NOC * NG
+UNITS = [(oc, g, 0, 4) for oc in range(NOC - 1) for g in range(NG)] + [(NOC - 1, g, 2 * h, 2) for h in range(2) for g in range(NG)]
+N_UNITS = len(UNITS)
 SCALE = 0.125
-LAG = 2
+LAG_BANKS = 4
 FLOPS = 2 * DO * DI * R + 2 * TOK * DI * DO
 
 
@@ -41,6 +42,7 @@ def tile_veralayer_pa_kernel(tc, x, A, B, d_A, d_B, out):
         out_v = out.rearrange("b s o -> (b s) o")
         a_v = A.rearrange("(p t) i -> p t i", t=4)
         b_v = B.rearrange("(c p j) r -> c p (j r)", p=P, j=4)
+        b_last = B[DO - CH : DO].rearrange("(h p j) r -> p h (j r)", h=2, j=2)
 
         ident_f = const.tile([P, P], F32, name="ident_f")
         da_b = const.tile([P, 4], BF16, name="da_b")
@@ -61,14 +63,20 @@ def tile_veralayer_pa_kernel(tc, x, A, B, d_A, d_B, out):
             elif kind == "x":
                 nc.sync.dma_start(out=x_raw[k][:], in_=x_v[:, :, 2 * k * CH : 2 * (k + 1) * CH])
             elif kind == "b":
-                nc.sync.dma_start(out=b_raw[k][:], in_=b_v[k])
+                if k == NOC - 1:
+                    nc.sync.dma_start(out=b_raw[k][:].rearrange("p (h w) -> p h w", h=2), in_=b_last)
+                else:
+                    pieces = 2 if k == 0 else 1
+                    w = 4 * R // pieces
+                    for u in range(pieces):
+                        nc.sync.dma_start(out=b_raw[k][:, w * u : w * u + w], in_=b_v[k][:, w * u : w * u + w])
             else:
                 nc.sync.dma_start(out=db_row[0:1, :], in_=d_B[0:CH].unsqueeze(0))
 
         nc.vector.memset(db_row[:].bitcast(I32), 0)
         nc.vector.memset(ones[:], 1.0)
         make_identity(nc, ident_f[:])
-        for kind, k in (("a", 0), ("da", 0), ("d", 0), ("b", 0), ("a", 1), ("x", 0), ("a", 2), ("x", 1), ("a", 3), ("b", 1), ("b", 2), ("b", 3)):
+        for kind, k in (("da", 0), ("a", 0), ("d", 0), ("b", 0), ("a", 1), ("x", 0), ("a", 2), ("x", 1), ("a", 3), ("b", 1), ("b", 2), ("b", 3)):
             load(kind, k)
         nc.sync.dma_start(out=db_rest[:], in_=d_B[CH:DO].partition_broadcast(P))
         nc.vector.tensor_copy(out=da_f[:], in_=da_b[:])
@@ -83,6 +91,9 @@ def tile_veralayer_pa_kernel(tc, x, A, B, d_A, d_B, out):
         scaled = {}
         grouped = {}
         acc = {}
+        todo = []
+        done = []
+        finished = []
 
         def words(kind, k, lo, hi):
             return codes[(kind, k)][0][:, lo:hi].bitcast(FP8X4)
@@ -96,11 +107,11 @@ def tile_veralayer_pa_kernel(tc, x, A, B, d_A, d_B, out):
             else:
                 nc.scalar.copy(out=dst, in_=src)
 
-        def scale_a(g):
+        def scale_a(g, eng):
             a_sc = grp.tile([P, 4, CH], BF16, name="a_sc", tag="a_sc")
             scaled[g] = a_sc
             for t in range(4):
-                nc.vector.tensor_scalar(
+                eng.tensor_scalar(
                     out=a_sc[:, t, :], in0=a_raw[g][:, t, :], scalar1=da_f[:, t : t + 1], scalar2=0.0, op0=MULT, op1=ADD
                 )
 
@@ -108,13 +119,23 @@ def tile_veralayer_pa_kernel(tc, x, A, B, d_A, d_B, out):
             if ("a", g) not in grouped:
                 ga = grp.tile([P, 4 * CH], BF16, name="ga", tag="grp", align_bytes=64)
                 grouped[("a", g)] = ga
+            if eng == "g":
+                nc.gpsimd.tensor_scalar(
+                    out=grouped[("a", g)][:].rearrange("p (q m t) -> p q m t", q=4, t=4)[:, :, r0 * 32 : r1 * 32],
+                    in0=scaled[g][:].rearrange("p t (m q) -> p q m t", q=4)[:, :, r0 * 32 : r1 * 32],
+                    scalar1=1.0,
+                    scalar2=0.0,
+                    op0=MULT,
+                    op1=ADD,
+                )
+                return
             copy_out(
                 eng,
                 grouped[("a", g)][:].rearrange("p (q m t) -> p m t q", q=4, t=4)[:, r0 * 32 : r1 * 32],
                 scaled[g][:].rearrange("p t (m q) -> p m t q", q=4)[:, r0 * 32 : r1 * 32],
             )
 
-        def transpose_half(kind, k, half, eng):
+        def transpose_half(kind, k, half, eng, tag=None):
             if kind == "x":
                 src = x_raw[k // 2][:].rearrange("p tt i -> p (tt i)").bitcast(F32)
                 row, w0 = CH, (k % 2) * (CH // 2)
@@ -125,7 +146,10 @@ def tile_veralayer_pa_kernel(tc, x, A, B, d_A, d_B, out):
                 gk = grp.tile([P, 4 * CH], BF16, name="gk", tag="grp", align_bytes=64)
                 grouped[(kind, k)] = gk
             gk32 = grouped[(kind, k)][:].bitcast(F32)
-            bank = ps_w.tile([P, 2, 2, P], F32, name="bank_t", tag="w")
+            if tag is None:
+                bank = ps_w.tile([P, 2, 2, P], F32, name="bank_t", tag="w")
+            else:
+                bank = ps_o.tile([P, 2, 2, P], F32, name="bank_t", tag=tag)
             for j in range(2):
                 for u in range(2):
                     w = (2 * half + j) * row + w0
@@ -146,13 +170,18 @@ def tile_veralayer_pa_kernel(tc, x, A, B, d_A, d_B, out):
                 in_=grouped[(kind, k)][:, 1024 * h : 1024 * (h + 1)],
             )
 
-        def w_bank(n, ob, m):
-            oc, g = n // NG, n % NG
-            if ob == 0:
-                wgv = wgp.tile([P, 4 * CH], BF16, name="wgv", tag="wgv", align_bytes=64)
-                wgg = wgp.tile([P, CH], BF16, name="wgg", tag="wgg", bufs=1, align_bytes=64)
-                grouped[("w", n)] = (wgv, wgg)
-            wgv, wgg = grouped[("w", n)]
+        def on_gpsimd(n, b):
+            return b == 0 and (UNITS[n][3] == 4 or UNITS[n][1] % 2 == 0)
+
+        def w_bank(n, b):
+            oc, g, lo, count = UNITS[n]
+            if b == 0:
+                wgv = wgp.tile([P, count * CH], BF16, name="wgv", tag="wgv", align_bytes=64)
+                grouped[("w", n)] = wgv
+                if on_gpsimd(n, 0):
+                    wgg = wgp.tile([P, CH], BF16, name="wgg", tag="wgg", bufs=1, align_bytes=64)
+                    grouped[("wg", n)] = wgg
+            ob = lo + b
             bank = ps_w.tile([P, 4, P], F32, name="bank_w", tag="w")
             for t in range(4):
                 nc.tensor.matmul_mx(
@@ -164,61 +193,87 @@ def tile_veralayer_pa_kernel(tc, x, A, B, d_A, d_B, out):
                     start=True,
                     stop=True,
                 )
-            if m is not None:
-                second_pass(m, ob)
-            db_chunk = db_first[:] if oc == 0 else db_rest[:, (oc - 1) * CH : oc * CH]
-            db = db_chunk.rearrange("p (o j) -> p j o", j=4)[:, ob].unsqueeze(2).to_broadcast([P, P, 4])
-            if ob == 0:
+            run_passes(n, CH)
+            db_unit = db_first[:] if oc == 0 else db_rest[:, (oc - 1) * CH + lo * P : (oc - 1) * CH + (lo + count) * P]
+            db = db_unit.rearrange("p (o j) -> p j o", j=count)[:, b].unsqueeze(2).to_broadcast([P, P, 4])
+            if on_gpsimd(n, b):
                 wf = wgp.tile([P, CH], F32, name="wf", tag="wf")
                 nc.scalar.copy(out=wf[:].rearrange("p (o t) -> p o t", t=4), in_=bank[:].rearrange("p t o -> p o t"))
                 nc.gpsimd.tensor_tensor(
-                    out=wgg[:].rearrange("p (o t) -> p o t", t=4),
+                    out=grouped[("wg", n)][:].rearrange("p (o t) -> p o t", t=4),
                     in0=wf[:].rearrange("p (o t) -> p o t", t=4),
                     in1=db,
                     op=MULT,
                 )
             else:
                 nc.vector.tensor_tensor(
-                    out=wgv[:, ob * CH : (ob + 1) * CH].rearrange("p (o t) -> p o t", t=4),
+                    out=grouped[("w", n)][:, b * CH : (b + 1) * CH].rearrange("p (o t) -> p o t", t=4),
                     in0=bank[:].rearrange("p t o -> p o t"),
                     in1=db,
                     op=MULT,
                 )
+
+        def run_passes(n, room):
+            while len(done) < len(todo) and room > 0:
+                m, tt = todo[len(done)]
+                if sum(u[3] for u in UNITS[m + 1 : n]) < LAG_BANKS:
+                    return
+                second_pass(m, tt)
+                done.append(m)
+                room -= UNITS[m][3] * P
+                if UNITS[m][1] == NG - 1:
+                    if UNITS[m][3] == 2:
+                        store_one(m, tt, "s")
+                    elif tt == 3:
+                        finished.append(m)
 
         def spread_d_b():
             bank = ps_o.tile([P, CH], F32, name="bank_d", tag="acc0")
             nc.tensor.matmul(out=bank[:], lhsT=ones[:], rhs=db_row[:], start=True, stop=True)
             nc.scalar.copy(out=db_first[:], in_=bank[:])
 
+        def quantise_w(n, lo, hi, src):
+            nc.vector.quantize_mx(out=words("w", n, lo, hi), scales=scales("w", n, lo, hi), in_=src)
+
         def w_quantise(n):
-            wgv, wgg = grouped[("w", n)]
-            for lo, hi, src in ((P, 3 * P, wgv[:, CH : 3 * CH]), (3 * P, 4 * P, wgv[:, 3 * CH : 4 * CH]), (0, P, wgg[:])):
-                nc.vector.quantize_mx(out=words("w", n, lo, hi), scales=scales("w", n, lo, hi), in_=src)
+            count = UNITS[n][3]
+            wgv = grouped[("w", n)]
+            if count == 4:
+                quantise_w(n, P, 3 * P, wgv[:, CH : 3 * CH])
+                quantise_w(n, 3 * P, 4 * P, wgv[:, 3 * CH : 4 * CH])
+                quantise_w(n, 0, P, grouped[("wg", n)][:])
+            elif not on_gpsimd(n, 0):
+                quantise_w(n - 1, 0, P, grouped[("wg", n - 1)][:])
+                quantise_w(n, 0, 2 * P, wgv[:])
 
         def second_pass(n, tt):
-            oc, g = n // NG, n % NG
+            oc, g, lo, count = UNITS[n]
+            w = count * P
             if g == 0:
-                acc[tt] = ps_o.tile([P, CH], F32, name="acc%d" % tt, tag="acc%d" % tt)
+                acc[tt] = ps_o.tile([P, w], F32, name="acc%d" % tt, tag="acc%d" % tt)
             nc.tensor.matmul_mx(
                 out=acc[tt][:],
                 lhsT=words("x", g, tt * P, (tt + 1) * P),
                 lhsT_scale=scales("x", g, tt * P, (tt + 1) * P),
-                rhs=words("w", n, 0, CH),
-                rhs_scale=scales("w", n, 0, CH),
+                rhs=words("w", n, 0, w),
+                rhs_scale=scales("w", n, 0, w),
                 start=(g == 0),
                 stop=(g == NG - 1),
             )
 
-        def store_out(oc, engs):
-            for tt in range(4):
-                o_sb = outp.tile([P, CH], F32, name="o_sb", tag="o_sb")
-                if engs[tt] == "v":
-                    nc.vector.tensor_scalar_mul(out=o_sb[:].rearrange("p (o j) -> p o j", j=4), in0=acc[tt][:].rearrange("p (j o) -> p o j", j=4), scalar1=SCALE)
-                else:
-                    nc.scalar.activation(out=o_sb[:].rearrange("p (o j) -> p o j", j=4), in_=acc[tt][:].rearrange("p (j o) -> p o j", j=4), func=COPY, scale=SCALE)
-                nc.sync.dma_start(out=out_v[tt * P : (tt + 1) * P, oc * CH : (oc + 1) * CH], in_=o_sb[:])
+        def store_one(n, tt, eng):
+            oc, g, lo, count = UNITS[n]
+            w = count * P
+            o_sb = outp.tile([P, w], F32, name="o_sb", tag="o_sb%d" % count, bufs=6 if count == 4 else 8)
+            dst = o_sb[:].rearrange("p (o j) -> p o j", j=count)
+            src = acc[tt][:].rearrange("p (j o) -> p o j", j=count)
+            if eng == "v":
+                nc.vector.tensor_scalar_mul(out=dst, in0=src, scalar1=SCALE)
+            else:
+                nc.scalar.activation(out=dst, in_=src, func=COPY, scale=SCALE)
+            nc.sync.dma_start(out=out_v[tt * P : (tt + 1) * P, oc * CH + lo * P : oc * CH + lo * P + w], in_=o_sb[:])
 
-        scale_a(0)
+        scale_a(0, nc.vector)
         regroup_a(0, 0, 3, "v")
         regroup_a(0, 3, 4, "s")
         for half in range(2):
@@ -227,28 +282,33 @@ def tile_veralayer_pa_kernel(tc, x, A, B, d_A, d_B, out):
         quantise("a", 0)
         quantise_half("b", 0, 0)
         quantise_half("b", 0, 1)
-        scale_a(1)
-        regroup_a(1, 0, 2, "v")
-        prepare = {0: [("x", 0), ("x", 1)], 1: [("x", 2), ("x", 3)], 2: [("b", 1), ("b", 2)], 3: [("b", 3)]}
+        scale_a(1, nc.vector)
+        regroup_a(1, 0, 1, "v")
+        prepare = {0: [("x", 0), ("x", 1)], 1: [("x", 2), ("x", 3)], 2: [("b", 1), ("b", 2)], 8: [("b", 3)]}
         for n in range(N_UNITS):
-            m = n - LAG if n >= LAG else None
-            for ob in range(4):
-                w_bank(n, ob, m)
-                if n + 1 < NG and (n > 0 or ob >= 2):
-                    regroup_a(n + 1, ob, ob + 1, "s")
-            for kind, k in prepare.get(n, []):
+            for b in range(UNITS[n][3]):
+                w_bank(n, b)
+                if UNITS[n][3] == 2 and b == 0 and not on_gpsimd(n, 0):
+                    quantise_w(n - 1, P, 2 * P, grouped[("w", n - 1)][:, CH : 2 * CH])
+                if n + 1 < NG and (n > 0 or b > 0):
+                    regroup_a(n + 1, b, b + 1, "s")
+            for i, (kind, k) in enumerate(prepare.get(n, [])):
                 for half in range(2):
-                    transpose_half(kind, k, half, "s")
+                    transpose_half(kind, k, half, "s", None)
             if n + 1 < NG:
                 quantise("a", n + 1)
             w_quantise(n)
+            for tt in range(4):
+                todo.append((n, tt))
             if n + 2 < NG:
-                scale_a(n + 2)
+                scale_a(n + 2, nc.vector)
             for kind, k in prepare.get(n, []):
                 quantise(kind, k)
-            if m is not None and m % NG == NG - 1:
-                store_out(m // NG, "ssss")
-        for m in range(N_UNITS - LAG, N_UNITS):
-            for tt in range(4):
-                second_pass(m, tt)
-        store_out(NOC - 1, "svsv")
+            for m in finished:
+                for tt in range(4):
+                    store_one(m, tt, "s")
+            finished.clear()
+        for m, tt in todo[len(done) :]:
+            second_pass(m, tt)
+            if UNITS[m][1] == NG - 1:
+                store_one(m, tt, "svsv"[tt])

from contextlib import ExitStack

import concourse.mybir as mybir
from concourse.masks import make_identity

F32 = mybir.dt.float32
BF16 = mybir.dt.bfloat16
U32 = mybir.dt.uint32
I32 = mybir.dt.int32
U8 = mybir.dt.uint8
FP8X4 = mybir.dt.float8_e4m3fn_x4
MULT = mybir.AluOpType.mult
ADD = mybir.AluOpType.add
COPY = mybir.ActivationFunctionType.Copy

P = 128
TOK, DI, DO, R = 512, 2048, 2048, 512
CH = 512
NG = DI // CH
NOC = DO // CH
UNITS = [(oc, g, 0, 4) for oc in range(NOC - 1) for g in range(NG)] + [(NOC - 1, g, 2 * h, 2) for h in range(2) for g in range(NG)]
N_UNITS = len(UNITS)
SCALE = 0.125
LAG_BANKS = 4
FLOPS = 2 * DO * DI * R + 2 * TOK * DI * DO


def tile_veralayer_pa_kernel(tc, x, A, B, d_A, d_B, out):
    nc = tc.nc
    with ExitStack() as ctx:
        ctx.enter_context(tc.manual_schedule())
        const = ctx.enter_context(tc.tile_pool(name="const", bufs=1))
        raw = ctx.enter_context(tc.tile_pool(name="raw", bufs=1))
        keep = ctx.enter_context(tc.tile_pool(name="keep", bufs=1))
        grp = ctx.enter_context(tc.tile_pool(name="grp", bufs=4))
        wgp = ctx.enter_context(tc.tile_pool(name="wgp", bufs=2))
        outp = ctx.enter_context(tc.tile_pool(name="outp", bufs=6))
        ps_w = ctx.enter_context(tc.psum_pool(name="ps_w", bufs=4))
        ps_o = ctx.enter_context(tc.psum_pool(name="ps_o", bufs=1))

        x_v = x.rearrange("b s i -> (b s) i").rearrange("(tt p) i -> p tt i", p=P)
        out_v = out.rearrange("b s o -> (b s) o")
        a_v = A.rearrange("(p t) i -> p t i", t=4)
        b_v = B.rearrange("(c p j) r -> c p (j r)", p=P, j=4)
        b_last = B[DO - CH : DO].rearrange("(h p j) r -> p h (j r)", h=2, j=2)

        ident_f = const.tile([P, P], F32, name="ident_f")
        da_b = const.tile([P, 4], BF16, name="da_b")
        da_f = const.tile([P, 4], F32, name="da_f")
        ones = const.tile([P, P], BF16, name="ones")
        db_row = const.tile([P, CH], BF16, name="db_row")
        db_first = const.tile([P, CH], BF16, name="db_first")
        db_rest = const.tile([P, DO - CH], BF16, name="db_rest")
        a_raw = [raw.tile([P, 4, CH], BF16, name="a_raw%d" % g) for g in range(NG)]
        x_raw = [raw.tile([P, 4, 2 * CH], BF16, name="x_raw%d" % h) for h in range(2)]
        b_raw = [raw.tile([P, 4 * R], BF16, name="b_raw%d" % c) for c in range(NOC)]

        def load(kind, k):
            if kind == "da":
                nc.sync.dma_start(out=da_b[:], in_=d_A.rearrange("(p t) -> p t", t=4))
            elif kind == "a":
                nc.sync.dma_start(out=a_raw[k][:], in_=a_v[:, :, k * CH : (k + 1) * CH])
            elif kind == "x":
                nc.sync.dma_start(out=x_raw[k][:], in_=x_v[:, :, 2 * k * CH : 2 * (k + 1) * CH])
            elif kind == "b":
                if k == NOC - 1:
                    nc.sync.dma_start(out=b_raw[k][:].rearrange("p (h w) -> p h w", h=2), in_=b_last)
                else:
                    pieces = 2 if k == 0 else 1
                    w = 4 * R // pieces
                    for u in range(pieces):
                        nc.sync.dma_start(out=b_raw[k][:, w * u : w * u + w], in_=b_v[k][:, w * u : w * u + w])
            else:
                nc.sync.dma_start(out=db_row[0:1, :], in_=d_B[0:CH].unsqueeze(0))

        nc.vector.memset(db_row[:].bitcast(I32), 0)
        nc.vector.memset(ones[:], 1.0)
        make_identity(nc, ident_f[:])
        for kind, k in (("da", 0), ("a", 0), ("d", 0), ("b", 0), ("a", 1), ("x", 0), ("a", 2), ("x", 1), ("a", 3), ("b", 1), ("b", 2), ("b", 3)):
            load(kind, k)
        nc.sync.dma_start(out=db_rest[:], in_=d_B[CH:DO].partition_broadcast(P))
        nc.vector.tensor_copy(out=da_f[:], in_=da_b[:])

        codes = {}
        for kind, count in (("a", NG), ("x", NG), ("b", NOC), ("w", N_UNITS)):
            for k in range(count):
                codes[(kind, k)] = (
                    keep.tile([P, CH], U32, name="%s_c%d" % (kind, k), align_bytes=64),
                    keep.tile([P, CH], U8, name="%s_s%d" % (kind, k), align_bytes=64),
                )
        scaled = {}
        grouped = {}
        acc = {}
        todo = []
        done = []
        finished = []

        def words(kind, k, lo, hi):
            return codes[(kind, k)][0][:, lo:hi].bitcast(FP8X4)

        def scales(kind, k, lo, hi):
            return codes[(kind, k)][1][:, lo:hi]

        def copy_out(eng, dst, src):
            if eng == "v":
                nc.vector.tensor_copy(out=dst, in_=src)
            else:
                nc.scalar.copy(out=dst, in_=src)

        def scale_a(g, eng):
            a_sc = grp.tile([P, 4, CH], BF16, name="a_sc", tag="a_sc")
            scaled[g] = a_sc
            for t in range(4):
                eng.tensor_scalar(
                    out=a_sc[:, t, :], in0=a_raw[g][:, t, :], scalar1=da_f[:, t : t + 1], scalar2=0.0, op0=MULT, op1=ADD
                )

        def regroup_a(g, r0, r1, eng):
            if ("a", g) not in grouped:
                ga = grp.tile([P, 4 * CH], BF16, name="ga", tag="grp", align_bytes=64)
                grouped[("a", g)] = ga
            if eng == "g":
                nc.gpsimd.tensor_scalar(
                    out=grouped[("a", g)][:].rearrange("p (q m t) -> p q m t", q=4, t=4)[:, :, r0 * 32 : r1 * 32],
                    in0=scaled[g][:].rearrange("p t (m q) -> p q m t", q=4)[:, :, r0 * 32 : r1 * 32],
                    scalar1=1.0,
                    scalar2=0.0,
                    op0=MULT,
                    op1=ADD,
                )
                return
            copy_out(
                eng,
                grouped[("a", g)][:].rearrange("p (q m t) -> p m t q", q=4, t=4)[:, r0 * 32 : r1 * 32],
                scaled[g][:].rearrange("p t (m q) -> p m t q", q=4)[:, r0 * 32 : r1 * 32],
            )

        def transpose_half(kind, k, half, eng, tag=None):
            if kind == "x":
                src = x_raw[k // 2][:].rearrange("p tt i -> p (tt i)").bitcast(F32)
                row, w0 = CH, (k % 2) * (CH // 2)
            else:
                src = b_raw[k][:].bitcast(F32)
                row, w0 = CH // 2, 0
            if (kind, k) not in grouped:
                gk = grp.tile([P, 4 * CH], BF16, name="gk", tag="grp", align_bytes=64)
                grouped[(kind, k)] = gk
            gk32 = grouped[(kind, k)][:].bitcast(F32)
            if tag is None:
                bank = ps_w.tile([P, 2, 2, P], F32, name="bank_t", tag="w")
            else:
                bank = ps_o.tile([P, 2, 2, P], F32, name="bank_t", tag=tag)
            for j in range(2):
                for u in range(2):
                    w = (2 * half + j) * row + w0
                    nc.tensor.transpose(bank[:, j, u, :], src[:, w + u : w + CH // 2 : 2], ident_f[:])
            copy_out(
                eng,
                gk32[:, half * CH : (half + 1) * CH].rearrange("p (j o u) -> p j o u", j=2, u=2),
                bank[:].rearrange("p j u o -> p j o u"),
            )

        def quantise(kind, k):
            nc.vector.quantize_mx(out=words(kind, k, 0, CH), scales=scales(kind, k, 0, CH), in_=grouped[(kind, k)][:])

        def quantise_half(kind, k, h):
            nc.vector.quantize_mx(
                out=words(kind, k, 256 * h, 256 * (h + 1)),
                scales=scales(kind, k, 256 * h, 256 * (h + 1)),
                in_=grouped[(kind, k)][:, 1024 * h : 1024 * (h + 1)],
            )

        def on_gpsimd(n, b):
            return b == 0 and (UNITS[n][3] == 4 or UNITS[n][1] % 2 == 0)

        def w_bank(n, b):
            oc, g, lo, count = UNITS[n]
            if b == 0:
                wgv = wgp.tile([P, count * CH], BF16, name="wgv", tag="wgv", align_bytes=64)
                grouped[("w", n)] = wgv
                if on_gpsimd(n, 0):
                    wgg = wgp.tile([P, CH], BF16, name="wgg", tag="wgg", bufs=1, align_bytes=64)
                    grouped[("wg", n)] = wgg
            ob = lo + b
            bank = ps_w.tile([P, 4, P], F32, name="bank_w", tag="w")
            for t in range(4):
                nc.tensor.matmul_mx(
                    out=bank[:, t, :],
                    lhsT=words("a", g, t * P, (t + 1) * P),
                    lhsT_scale=scales("a", g, t * P, (t + 1) * P),
                    rhs=words("b", oc, ob * P, (ob + 1) * P),
                    rhs_scale=scales("b", oc, ob * P, (ob + 1) * P),
                    start=True,
                    stop=True,
                )
            run_passes(n, CH)
            db_unit = db_first[:] if oc == 0 else db_rest[:, (oc - 1) * CH + lo * P : (oc - 1) * CH + (lo + count) * P]
            db = db_unit.rearrange("p (o j) -> p j o", j=count)[:, b].unsqueeze(2).to_broadcast([P, P, 4])
            if on_gpsimd(n, b):
                wf = wgp.tile([P, CH], F32, name="wf", tag="wf")
                nc.scalar.copy(out=wf[:].rearrange("p (o t) -> p o t", t=4), in_=bank[:].rearrange("p t o -> p o t"))
                nc.gpsimd.tensor_tensor(
                    out=grouped[("wg", n)][:].rearrange("p (o t) -> p o t", t=4),
                    in0=wf[:].rearrange("p (o t) -> p o t", t=4),
                    in1=db,
                    op=MULT,
                )
            else:
                nc.vector.tensor_tensor(
                    out=grouped[("w", n)][:, b * CH : (b + 1) * CH].rearrange("p (o t) -> p o t", t=4),
                    in0=bank[:].rearrange("p t o -> p o t"),
                    in1=db,
                    op=MULT,
                )

        def run_passes(n, room):
            while len(done) < len(todo) and room > 0:
                m, tt = todo[len(done)]
                if sum(u[3] for u in UNITS[m + 1 : n]) < LAG_BANKS:
                    return
                second_pass(m, tt)
                done.append(m)
                room -= UNITS[m][3] * P
                if UNITS[m][1] == NG - 1:
                    if UNITS[m][3] == 2:
                        store_one(m, tt, "s")
                    elif tt == 3:
                        finished.append(m)

        def spread_d_b():
            bank = ps_o.tile([P, CH], F32, name="bank_d", tag="acc0")
            nc.tensor.matmul(out=bank[:], lhsT=ones[:], rhs=db_row[:], start=True, stop=True)
            nc.scalar.copy(out=db_first[:], in_=bank[:])

        def quantise_w(n, lo, hi, src):
            nc.vector.quantize_mx(out=words("w", n, lo, hi), scales=scales("w", n, lo, hi), in_=src)

        def w_quantise(n):
            count = UNITS[n][3]
            wgv = grouped[("w", n)]
            if count == 4:
                quantise_w(n, P, 3 * P, wgv[:, CH : 3 * CH])
                quantise_w(n, 3 * P, 4 * P, wgv[:, 3 * CH : 4 * CH])
                quantise_w(n, 0, P, grouped[("wg", n)][:])
            elif not on_gpsimd(n, 0):
                quantise_w(n - 1, 0, P, grouped[("wg", n - 1)][:])
                quantise_w(n, 0, 2 * P, wgv[:])

        def second_pass(n, tt):
            oc, g, lo, count = UNITS[n]
            w = count * P
            if g == 0:
                acc[tt] = ps_o.tile([P, w], F32, name="acc%d" % tt, tag="acc%d" % tt)
            nc.tensor.matmul_mx(
                out=acc[tt][:],
                lhsT=words("x", g, tt * P, (tt + 1) * P),
                lhsT_scale=scales("x", g, tt * P, (tt + 1) * P),
                rhs=words("w", n, 0, w),
                rhs_scale=scales("w", n, 0, w),
                start=(g == 0),
                stop=(g == NG - 1),
            )

        def store_one(n, tt, eng):
            oc, g, lo, count = UNITS[n]
            w = count * P
            o_sb = outp.tile([P, w], F32, name="o_sb", tag="o_sb%d" % count, bufs=6 if count == 4 else 8)
            dst = o_sb[:].rearrange("p (o j) -> p o j", j=count)
            src = acc[tt][:].rearrange("p (j o) -> p o j", j=count)
            if eng == "v":
                nc.vector.tensor_scalar_mul(out=dst, in0=src, scalar1=SCALE)
            else:
                nc.scalar.activation(out=dst, in_=src, func=COPY, scale=SCALE)
            nc.sync.dma_start(out=out_v[tt * P : (tt + 1) * P, oc * CH + lo * P : oc * CH + lo * P + w], in_=o_sb[:])

        scale_a(0, nc.vector)
        regroup_a(0, 0, 3, "v")
        regroup_a(0, 3, 4, "s")
        for half in range(2):
            transpose_half("b", 0, half, "s")
        spread_d_b()
        quantise("a", 0)
        quantise_half("b", 0, 0)
        quantise_half("b", 0, 1)
        scale_a(1, nc.vector)
        regroup_a(1, 0, 1, "v")
        prepare = {0: [("x", 0), ("x", 1)], 1: [("x", 2), ("x", 3)], 2: [("b", 1), ("b", 2)], 8: [("b", 3)]}
        for n in range(N_UNITS):
            for b in range(UNITS[n][3]):
                w_bank(n, b)
                if UNITS[n][3] == 2 and b == 0 and not on_gpsimd(n, 0):
                    quantise_w(n - 1, P, 2 * P, grouped[("w", n - 1)][:, CH : 2 * CH])
                if n + 1 < NG and (n > 0 or b > 0):
                    regroup_a(n + 1, b, b + 1, "s")
            for i, (kind, k) in enumerate(prepare.get(n, [])):
                for half in range(2):
                    transpose_half(kind, k, half, "s", None)
            if n + 1 < NG:
                quantise("a", n + 1)
            w_quantise(n)
            for tt in range(4):
                todo.append((n, tt))
            if n + 2 < NG:
                scale_a(n + 2, nc.vector)
            for kind, k in prepare.get(n, []):
                quantise(kind, k)
            for m in finished:
                for tt in range(4):
                    store_one(m, tt, "s")
            finished.clear()
        for m, tt in todo[len(done) :]:
            second_pass(m, tt)
            if UNITS[m][1] == NG - 1:
                store_one(m, tt, "svsv"[tt])
